import numpy as np
import ml_dtypes


def mxq(x, axis, fmt="e4m3"):
    dtype, down = {"e4m3": (ml_dtypes.float8_e4m3fn, 7), "e5m2": (ml_dtypes.float8_e5m2, 14)}[fmt]
    v = np.moveaxis(np.asarray(x, np.float32).astype(ml_dtypes.bfloat16).astype(np.float64), axis, -1)
    blocks = v.reshape(v.shape[:-1] + (-1, 32))
    amax = np.abs(blocks).max(-1, keepdims=True)
    byte = np.maximum(np.where(amax > 0, np.frexp(amax)[1] - 1 + 127, 0) - down, 1)
    scale = np.exp2(byte - 127.0)
    codes = (blocks / scale).astype(np.float32).astype(dtype).astype(np.float64)
    return np.moveaxis((codes * scale).reshape(v.shape), -1, axis)


WIDE = False


def mx_kscale(k):
    if not WIDE:
        return np.ones(k)
    levels = np.array([10, -10, 5, -5, 0])
    if k % 512:
        return np.exp2(np.random.permutation(np.resize(levels, k // 32))).repeat(32)
    a = np.empty((k // 512, 16))
    for p in range(k // 512):
        a[p, :8] = np.random.permutation(np.resize(levels, 8))
        for g in range(8):
            far = levels[np.abs(levels - a[p, g]) >= 10]
            a[p, g + 8] = far[np.random.randint(len(far))]
    return np.exp2(a.ravel()).repeat(32)


BF16 = ml_dtypes.bfloat16


def bf(x):
    return np.asarray(x, np.float32).astype(BF16)


def f64(x):
    return np.asarray(x).astype(np.float64)


B, H, W, C = 128, 5, 5, 1024
G = C // 4
NBR = 3


def setup_inputs():
    s = mx_kscale(C)
    return {
        "h_mix": bf(0.8 * np.random.standard_normal((B, H, W, C)) * s),
        "w_mix": bf(0.8 * np.random.standard_normal((B, H, W, C)) * s),
        "c_proj": bf(np.random.standard_normal((B, H, W, C)) * s),
        "gate_hid": bf(0.6 * np.random.standard_normal((B, G))),
        "wa2": bf(2.0 * np.random.standard_normal((G, C * NBR)) / np.sqrt(G)),
        "ba2": bf(0.6 * np.random.standard_normal(C * NBR)),
        "wo": bf(np.random.standard_normal((C, C)) / np.sqrt(C) / s[:, None]),
        "bo": bf(0.3 * np.random.standard_normal(C)),
    }


def reference(h_mix, w_mix, c_proj, gate_hid, wa2, ba2, wo, bo):
    z = f64(gate_hid) @ f64(wa2) + f64(ba2)
    z = z.reshape(B, C, NBR).transpose(2, 0, 1)
    e = np.exp(z - z.max(0, keepdims=True))
    a = (e / e.sum(0, keepdims=True))[:, :, None, None, :]
    fused = f64(h_mix) * a[0] + f64(w_mix) * a[1] + f64(c_proj) * a[2]
    return (mxq(fused, 3, "e4m3") @ mxq(f64(wo), 0, "e4m3")) + f64(bo)

@@ -1,0 +1,295 @@
+from contextlib import ExitStack
+
+import concourse.mybir as mybir
+from concourse.masks import make_identity
+
+F32 = mybir.dt.float32
+BF16 = mybir.dt.bfloat16
+U32 = mybir.dt.uint32
+U8 = mybir.dt.uint8
+FP8X4 = mybir.dt.float8_e4m3fn_x4
+ALU = mybir.AluOpType
+ACT = mybir.ActivationFunctionType
+
+P = 128
+B, HW, C, GH, NBR = 128, 25, 1024, 256, 3
+HALF = 512
+XBUFS = 3
+CHUNKS = ((0, 2), (2, 4), (6, 4), (10, 4), (14, 4), (18, 4), (22, 3))
+BLOCKS = ((0, 1), (1, 1)) + tuple((2 + 2 * i, 2) for i in range(11)) + ((24, 1),)
+NB = len(BLOCKS)
+
+FLOPS = 2 * B * HW * C * C + 2 * B * GH * NBR * C
+
+
+def by_fours(ap):
+    return ap.rearrange("b n (r t) -> b n t r", t=4)
+
+
+def in_runs(ap):
+    return ap.rearrange("b n (t r) -> b n t r", t=4)
+
+
+def tile_hiremodule_pc_kernel(tc, h_mix, w_mix, c_proj, gate_hid, wa2, ba2, wo, bo, out):
+    nc = tc.nc
+    xv = [x.rearrange("b i j c -> b (i j) c") for x in (h_mix, w_mix, c_proj)]
+    outv = out.rearrange("b i j c -> b (i j) c")
+
+    with ExitStack() as ctx:
+        ctx.enter_context(tc.manual_schedule())
+        consts = ctx.enter_context(tc.tile_pool(name="consts", bufs=1))
+        xpool = ctx.enter_context(tc.tile_pool(name="xpool", bufs=XBUFS))
+        ppool = ctx.enter_context(tc.tile_pool(name="ppool", bufs=2))
+        gpool = ctx.enter_context(tc.tile_pool(name="gpool", bufs=2))
+        psum = ctx.enter_context(tc.psum_pool(name="psum", bufs=1))
+
+        ident_f = consts.tile([P, P], F32, name="ident_f")
+        ident_b = consts.tile([P, P], BF16, name="ident_b")
+        a_sb = consts.tile([P, NBR, C], F32, name="a_sb")
+        bo_bc = consts.tile([P, C], BF16, name="bo_bc")
+        w_codes = consts.tile([P, 2, C], U32, name="w_codes", align_bytes=64)
+        w_scales = consts.tile([P, 2, C], U8, name="w_scales", align_bytes=64)
+
+        xt = {}
+        a_ps = {}
+        prod = {}
+        quant = {}
+        stage = {}
+        pools = {}
+
+        def load_chunk(c):
+            i0, cn = CHUNKS[c]
+            for k in range(NBR):
+                t = xpool.tile([P, cn, C], BF16, tag="x%d" % k, name="x%d_%d" % (k, c))
+                nc.sync.dma_start(out=t[:], in_=xv[k][:, i0:i0 + cn, :])
+                xt[(k, c)] = t
+
+        def load_after(q):
+            ij_end = BLOCKS[q][0] + BLOCKS[q][1]
+            for c in range(len(CHUNKS) - XBUFS):
+                if CHUNKS[c][0] + CHUNKS[c][1] == ij_end:
+                    load_chunk(c + XBUFS)
+
+        def where(ij):
+            for c in range(len(CHUNKS)):
+                i0, cn = CHUNKS[c]
+                if i0 <= ij < i0 + cn:
+                    return c, ij - i0
+            return None
+
+        def new_products(q):
+            n = BLOCKS[q][1]
+            for k in range(NBR):
+                prod[(q, k)] = ppool.tile([P, n, C], F32, tag="p%d" % k, name="p%d_%d" % (k, q))
+
+        def pre_added(q):
+            return BLOCKS[q][1] == 2
+
+        def halves(q):
+            return (1, 0) if pre_added(q) else (0, 1)
+
+        def touch(q):
+            first = halves(q)[0] * HALF
+            nc.vector.memset(prod[(q, 2)][:, 0, first:first + 8], 0.0)
+
+        def gpsimd_share(q):
+            n = BLOCKS[q][1]
+            c, j0 = where(BLOCKS[q][0])
+            for hf in halves(q):
+                hs = slice(hf * HALF, (hf + 1) * HALF)
+                nc.gpsimd.tensor_tensor(
+                    out=in_runs(prod[(q, 2)][:, :, hs]), in0=by_fours(xt[(2, c)][:, j0:j0 + n, hs]),
+                    in1=in_runs(a_sb[:, 2, hs].unsqueeze(1).to_broadcast([P, n, HALF])), op=ALU.mult)
+
+        def gpsimd_add(q):
+            if pre_added(q):
+                nc.gpsimd.tensor_tensor(out=prod[(q, 2)][:, :, 0:HALF], in0=prod[(q, 2)][:, :, 0:HALF],
+                                        in1=prod[(q, 1)][:, :, 0:HALF], op=ALU.add)
+
+        def vector_share(q):
+            n = BLOCKS[q][1]
+            c, j0 = where(BLOCKS[q][0])
+            for (k, hf) in [(k, hf) for hf in halves(q) for k in (1, 0)]:
+                hs = slice(hf * HALF, (hf + 1) * HALF)
+                nc.vector.tensor_tensor(
+                    out=in_runs(prod[(q, k)][:, :, hs]), in0=by_fours(xt[(k, c)][:, j0:j0 + n, hs]),
+                    in1=in_runs(a_ps[(k, hf)][:].unsqueeze(1).to_broadcast([P, n, HALF])), op=ALU.mult)
+
+        def t_run(q, jj, g):
+            n = BLOCKS[q][1]
+            if q not in quant:
+                quant[q] = (
+                    gpool.tile([P, n, 2, P, 4], BF16, tag="grp", name="grp%d" % q, align_bytes=64),
+                    gpool.tile([P, n * 2 * P], U32, tag="codes", name="codes%d" % q, align_bytes=64),
+                    gpool.tile([P, n * 2 * P], U8, tag="scl", name="scl%d" % q, align_bytes=64),
+                )
+            acc = psum.tile([P, 4, P], F32, tag="acc", name="acc%d_%d_%d" % (g, q, jj), bufs=2)
+            srcs = (2, 0) if (g == 0 and pre_added(q)) else (2, 1, 0)
+            for t in range(4):
+                col = (4 * g + t) * P
+                for k in srcs:
+                    nc.tensor.matmul(acc[:, t, :], lhsT=prod[(q, k)][:, jj, col:col + P], rhs=ident_f[:],
+                                     is_transpose=True, start=(k == 2), stop=(k == 0))
+            nc.scalar.copy(out=quant[q][0][:, jj, g, :, :], in_=acc[:].rearrange("p t b -> p b t"))
+
+        def quantise(q):
+            grp, codes, scl = quant[q]
+            nc.vector.quantize_mx(out=codes[:].bitcast(FP8X4), scales=scl[:],
+                                  in_=grp[:].rearrange("p j g b t -> p (j g b t)"))
+
+        def mx_pair(q, jj, nh):
+            codes, scl = quant[q][1], quant[q][2]
+            ns = slice(nh * HALF, (nh + 1) * HALF)
+            o = psum.tile([P, HALF], F32, tag="o", name="o%d_%d_%d" % (nh, q, jj), bufs=2)
+            for g in range(2):
+                gs = slice((2 * jj + g) * P, (2 * jj + g + 1) * P)
+                nc.tensor.matmul_mx(
+                    out=o[:], lhsT=codes[:, gs].bitcast(FP8X4), lhsT_scale=scl[:, gs],
+                    rhs=w_codes[:, g, ns].bitcast(FP8X4), rhs_scale=w_scales[:, g, ns],
+                    start=(g == 0), stop=(g == 1))
+            return o
+
+        def add_bias(q, jj, nh, o):
+            ij0, n = BLOCKS[q]
+            if (jj, nh) == (0, 0):
+                stage[q] = pools["o"].tile([P, n, C], F32, tag="ost", name="ost%d" % q)
+            ns = slice(nh * HALF, (nh + 1) * HALF)
+            nc.vector.tensor_tensor(out=stage[q][:, jj, ns], in0=o[:], in1=bo_bc[:, ns], op=ALU.add)
+            if (jj, nh) == (n - 1, 1):
+                nc.sync.dma_start(out=outv[:, ij0:ij0 + n, :], in_=stage[q][:])
+
+        z_tags = (("pa", "pb"), ("pc", "pd"), ("o", "o"))
+
+        with tc.tile_pool(name="head", bufs=1) as head:
+            make_identity(nc, ident_b[:])
+            make_identity(nc, ident_f[:])
+
+            ba_rows = head.tile([P, NBR * C], BF16, name="ba_rows")
+            nc.vector.memset(ba_rows[:], 0.0)
+            ones_b = head.tile([P, P], BF16, name="ones_b")
+            nc.vector.memset(ones_b[:], 1.0)
+            warm = head.tile([P, 1], F32, name="warm")
+            nc.vector.memset(warm[:], 0.0)
+
+            gh = head.tile([P, GH], BF16, name="gh")
+            nc.sync.dma_start(out=gh[:], in_=gate_hid)
+            nc.sync.dma_start(out=ba_rows[0:1, :], in_=ba2.rearrange("(o c) -> o c", o=1))
+            wa = head.tile([P, 2, NBR * C], BF16, tag="wa", name="wa", align_bytes=64)
+            wav = wa2.rearrange("(kc p) c -> p kc c", p=P)
+            for hf in range(2):
+                cols = slice(hf * NBR * HALF, (hf + 1) * NBR * HALF)
+                nc.sync.dma_start(out=wa[:, :, cols], in_=wav[:, :, cols])
+            wo_raw = head.tile([P, 2, 4, C], BF16, name="wo_raw")
+            nc.sync.dma_start(out=wo_raw[:], in_=wo.rearrange("(g p t) n -> p g t n", g=2, t=4, p=P))
+            for c in range(XBUFS):
+                load_chunk(c)
+            nc.sync.dma_start(out=bo_bc[:], in_=bo.partition_broadcast(P))
+
+            nc.scalar.activation(out=warm[:], in_=warm[:], func=ACT.Exp)
+
+            ght_ps = psum.tile([P, 2, P], BF16, tag="acc", name="ght_ps", bufs=2)
+            for kc in range(2):
+                nc.tensor.transpose(ght_ps[:, kc, :], gh[:, kc * P:(kc + 1) * P], ident_b[:])
+            ght = head.tile([P, 2, P], BF16, name="ght")
+            nc.vector.tensor_copy(out=ght[:], in_=ght_ps[:])
+
+            z = {}
+            for hf in range(2):
+                cols = slice(hf * NBR * HALF, (hf + 1) * NBR * HALF)
+                for k in range(NBR):
+                    zt = psum.tile([P, HALF], F32, tag=z_tags[k][hf], name="z%d_%d" % (k, hf),
+                                   bufs=(2 if z_tags[k][hf] == "o" else 1))
+                    nc.tensor.matmul(
+                        zt[:].rearrange("p (t r) -> p t r", t=4), lhsT=ones_b[:],
+                        rhs=ba_rows[:, cols].rearrange("p (r t k) -> p k t r", t=4, k=NBR)[:, k],
+                        start=True, stop=False)
+                    z[(k, hf)] = zt
+                for k in range(NBR):
+                    for kc in range(2):
+                        nc.tensor.matmul(
+                            z[(k, hf)][:].rearrange("p (t r) -> p t r", t=4), lhsT=ght[:, kc, :],
+                            rhs=wa[:, kc, cols].rearrange("p (r t k) -> p k t r", t=4, k=NBR)[:, k],
+                            start=False, stop=(kc == 1))
+
+            wo_grp = [head.tile([P, C, 4], BF16, tag="wa", name="wo_grp0", align_bytes=64),
+                      head.tile([P, C, 4], BF16, name="wo_grp1", align_bytes=64)]
+            for piece in range(4):
+                ns = slice(piece * 256, (piece + 1) * 256)
+                nc.gpsimd.tensor_scalar(out=wo_grp[1][:, ns, :],
+                                        in0=wo_raw[:, 1, :, ns].rearrange("p t n -> p n t"),
+                                        scalar1=1.0, scalar2=0.0, op0=ALU.mult, op1=ALU.add)
+
+            e = {}
+            s = {}
+            y = {}
+            mx = {}
+            for hf in range(2):
+                mx[hf] = head.tile([P, HALF], F32, name="m_%d" % hf)
+                nc.scalar.copy(out=mx[hf][:], in_=z[(0, hf)][:])
+            for hf in range(2):
+                m = mx[hf]
+                nc.vector.tensor_tensor(out=m[:], in0=z[(1, hf)][:], in1=m[:], op=ALU.max)
+                nc.vector.tensor_tensor(out=m[:], in0=z[(2, hf)][:], in1=m[:], op=ALU.max)
+                e[hf] = head.tile([P, NBR, HALF], F32, name="e_%d" % hf)
+                for k in range(NBR):
+                    nc.vector.tensor_tensor(out=e[hf][:, k, :], in0=z[(k, hf)][:], in1=m[:], op=ALU.subtract)
+                nc.scalar.activation(out=e[hf][:], in_=e[hf][:], func=ACT.Exp)
+            for hf in range(2):
+                s[hf] = head.tile([P, HALF], F32, name="s_%d" % hf)
+                y[hf] = head.tile([P, HALF], F32, name="y_%d" % hf)
+                nc.vector.tensor_tensor(out=s[hf][:], in0=e[hf][:, 0, :], in1=e[hf][:, 1, :], op=ALU.add)
+                nc.vector.tensor_tensor(out=s[hf][:], in0=s[hf][:], in1=e[hf][:, 2, :], op=ALU.add)
+            for hf in range(2):
+                nc.scalar.activation(out=y[hf][:], in_=s[hf][:], func=ACT.Abs_reciprocal_sqrt)
+                nc.scalar.activation(out=y[hf][:], in_=y[hf][:], func=ACT.Square)
+            nc.vector.quantize_mx(out=w_codes[:, 1, :].bitcast(FP8X4), scales=w_scales[:, 1, :],
+                                  in_=wo_grp[1][:].rearrange("p n t -> p (n t)"))
+            for piece in range(4):
+                ns = slice(piece * 256, (piece + 1) * 256)
+                nc.scalar.copy(out=wo_grp[0][:, ns, :], in_=wo_raw[:, 0, :, ns].rearrange("p t n -> p n t"))
+
+            for hf in range(2):
+                hs = slice(hf * HALF, (hf + 1) * HALF)
+                nc.vector.tensor_tensor(out=s[hf][:], in0=s[hf][:], in1=y[hf][:], op=ALU.mult)
+                nc.vector.scalar_tensor_tensor(out=y[hf][:], in0=s[hf][:], scalar=2.0, in1=y[hf][:],
+                                               op0=ALU.subtract, op1=ALU.mult)
+                nc.vector.scalar_tensor_tensor(
+                    out=a_sb[:, :, hs], in0=e[hf][:], scalar=-1.0,
+                    in1=y[hf][:].unsqueeze(1).to_broadcast([P, NBR, HALF]), op0=ALU.mult, op1=ALU.mult)
+                for k in (1, 0):
+                    ap = psum.tile([P, HALF], F32, tag=z_tags[k][hf], name="aps%d_%d" % (k, hf))
+                    nc.tensor.matmul(ap[:], lhsT=ident_f[:], rhs=a_sb[:, k, hs], start=True, stop=True)
+                    a_ps[(k, hf)] = ap
+
+            for q in range(2):
+                new_products(q)
+                gpsimd_share(q)
+            for q in range(2):
+                vector_share(q)
+                gpsimd_add(q)
+                load_after(q)
+            nc.vector.quantize_mx(out=w_codes[:, 0, :].bitcast(FP8X4), scales=w_scales[:, 0, :],
+                                  in_=wo_grp[0][:].rearrange("p n t -> p (n t)"))
+
+        pools["o"] = ctx.enter_context(tc.tile_pool(name="opool", bufs=3))
+
+        for q in range(NB + 1):
+            if q < NB:
+                for g in halves(q):
+                    for jj in range(BLOCKS[q][1]):
+                        t_run(q, jj, g)
+            pairs = [(jj, nh) for jj in range(BLOCKS[q - 1][1]) for nh in range(2)] if q >= 1 else []
+            for (jj, nh) in pairs[:2]:
+                add_bias(q - 1, jj, nh, mx_pair(q - 1, jj, nh))
+            if q < NB:
+                quantise(q)
+            if q + 2 < NB:
+                new_products(q + 2)
+                touch(q + 2)
+                gpsimd_share(q + 2)
+            for (jj, nh) in pairs[2:]:
+                add_bias(q - 1, jj, nh, mx_pair(q - 1, jj, nh))
+            if q + 2 < NB:
+                vector_share(q + 2)
+                gpsimd_add(q + 2)
+                load_after(q + 2)

@@ -22,12 +22,17 @@ NB = len(BLOCKS)
 FLOPS = 2 * B * HW * C * C + 2 * B * GH * NBR * C
 
 
-def by_fours(ap):
-    return ap.rearrange("b n (r t) -> b n t r", t=4)
+def by_channel(ap, hf):
+    return ap.rearrange("b n (q t r) -> b t n q r", t=4, r=8)[:, 2 * hf:2 * hf + 2]
 
 
-def in_runs(ap):
-    return ap.rearrange("b n (t r) -> b n t r", t=4)
+def by_parts(t, hf):
+    return t[:, 2 * hf:2 * hf + 2].rearrange("b t n (q r) -> b t n q r", r=8)
+
+
+def over_images(ap, n):
+    v = ap.rearrange("b (t q r) -> b t q r", t=2, r=8).unsqueeze(2)
+    return v.to_broadcast([P, 2, n, 32, 8])
 
 
 def tile_hiremodule_pc_kernel(tc, h_mix, w_mix, c_proj, gate_hid, wa2, ba2, wo, bo, out):
@@ -80,7 +85,7 @@ def tile_hiremodule_pc_kernel(tc, h_mix, w_mix, c_proj, gate_hid, wa2, ba2, wo, 
         def new_products(q):
             n = BLOCKS[q][1]
             for k in range(NBR):
-                prod[(q, k)] = ppool.tile([P, n, C], F32, tag="p%d" % k, name="p%d_%d" % (k, q))
+                prod[(q, k)] = ppool.tile([P, 4, n, C // 4], F32, tag="p%d" % k, name="p%d_%d" % (k, q))
 
         def pre_added(q):
             return BLOCKS[q][1] == 2
@@ -89,31 +94,28 @@ def tile_hiremodule_pc_kernel(tc, h_mix, w_mix, c_proj, gate_hid, wa2, ba2, wo, 
             return (1, 0) if pre_added(q) else (0, 1)
 
         def touch(q):
-            first = halves(q)[0] * HALF
-            nc.vector.memset(prod[(q, 2)][:, 0, first:first + 8], 0.0)
+            nc.vector.memset(prod[(q, 2)][:, 2 * halves(q)[0], 0, 0:8], 0.0)
 
         def gpsimd_share(q):
             n = BLOCKS[q][1]
             c, j0 = where(BLOCKS[q][0])
             for hf in halves(q):
-                hs = slice(hf * HALF, (hf + 1) * HALF)
                 nc.gpsimd.tensor_tensor(
-                    out=in_runs(prod[(q, 2)][:, :, hs]), in0=by_fours(xt[(2, c)][:, j0:j0 + n, hs]),
-                    in1=in_runs(a_sb[:, 2, hs].unsqueeze(1).to_broadcast([P, n, HALF])), op=ALU.mult)
+                    out=by_parts(prod[(q, 2)], hf), in0=by_channel(xt[(2, c)][:, j0:j0 + n, :], hf),
+                    in1=over_images(a_sb[:, 2, hf * HALF:(hf + 1) * HALF], n), op=ALU.mult)
 
         def gpsimd_add(q):
             if pre_added(q):
-                nc.gpsimd.tensor_tensor(out=prod[(q, 2)][:, :, 0:HALF], in0=prod[(q, 2)][:, :, 0:HALF],
-                                        in1=prod[(q, 1)][:, :, 0:HALF], op=ALU.add)
+                nc.gpsimd.tensor_tensor(out=prod[(q, 2)][:, 0:2], in0=prod[(q, 2)][:, 0:2],
+                                        in1=prod[(q, 1)][:, 0:2], op=ALU.add)
 
         def vector_share(q):
             n = BLOCKS[q][1]
             c, j0 = where(BLOCKS[q][0])
             for (k, hf) in [(k, hf) for hf in halves(q) for k in (1, 0)]:
-                hs = slice(hf * HALF, (hf + 1) * HALF)
                 nc.vector.tensor_tensor(
-                    out=in_runs(prod[(q, k)][:, :, hs]), in0=by_fours(xt[(k, c)][:, j0:j0 + n, hs]),
-                    in1=in_runs(a_ps[(k, hf)][:].unsqueeze(1).to_broadcast([P, n, HALF])), op=ALU.mult)
+                    out=by_parts(prod[(q, k)], hf), in0=by_channel(xt[(k, c)][:, j0:j0 + n, :], hf),
+                    in1=over_images(a_ps[(k, hf)][:], n), op=ALU.mult)
 
         def t_run(q, jj, g):
             n = BLOCKS[q][1]
@@ -124,11 +126,9 @@ def tile_hiremodule_pc_kernel(tc, h_mix, w_mix, c_proj, gate_hid, wa2, ba2, wo, 
                     gpool.tile([P, n * 2 * P], U8, tag="scl", name="scl%d" % q, align_bytes=64),
                 )
             acc = psum.tile([P, 4, P], F32, tag="acc", name="acc%d_%d_%d" % (g, q, jj), bufs=2)
-            srcs = (2, 0) if (g == 0 and pre_added(q)) else (2, 1, 0)
-            for t in range(4):
-                col = (4 * g + t) * P
-                for k in srcs:
-                    nc.tensor.matmul(acc[:, t, :], lhsT=prod[(q, k)][:, jj, col:col + P], rhs=ident_f[:],
+            for t in (2, 3, 0, 1) if pre_added(q) else (0, 1, 2, 3):
+                for k in (2, 0) if (t < 2 and pre_added(q)) else (2, 1, 0):
+                    nc.tensor.matmul(acc[:, t, :], lhsT=prod[(q, k)][:, t, jj, g * P:(g + 1) * P], rhs=ident_f[:],
                                      is_transpose=True, start=(k == 2), stop=(k == 0))
             nc.scalar.copy(out=quant[q][0][:, jj, g, :, :], in_=acc[:].rearrange("p t b -> p b t"))
 
@@ -180,7 +180,10 @@ def tile_hiremodule_pc_kernel(tc, h_mix, w_mix, c_proj, gate_hid, wa2, ba2, wo, 
                 cols = slice(hf * NBR * HALF, (hf + 1) * NBR * HALF)
                 nc.sync.dma_start(out=wa[:, :, cols], in_=wav[:, :, cols])
             wo_raw = head.tile([P, 2, 4, C], BF16, name="wo_raw")
-            nc.sync.dma_start(out=wo_raw[:], in_=wo.rearrange("(g p t) n -> p g t n", g=2, t=4, p=P))
+            wov = wo.rearrange("(g q t r) n -> r g q t n", g=2, t=4, r=8)
+            for g in range(2):
+                for r in (0, 4, 1, 5, 2, 6, 3, 7):
+                    nc.sync.dma_start(out=wo_raw[r:P:8, g, :, :], in_=wov[r, g])
             for c in range(XBUFS):
                 load_chunk(c)
             nc.sync.dma_start(out=bo_bc[:], in_=bo.partition_broadcast(P))
@@ -195,20 +198,20 @@ def tile_hiremodule_pc_kernel(tc, h_mix, w_mix, c_proj, gate_hid, wa2, ba2, wo, 
 
             z = {}
             for hf in range(2):
-                cols = slice(hf * NBR * HALF, (hf + 1) * NBR * HALF)
+                ts = slice(2 * hf, 2 * hf + 2)
                 for k in range(NBR):
                     zt = psum.tile([P, HALF], F32, tag=z_tags[k][hf], name="z%d_%d" % (k, hf),
                                    bufs=(2 if z_tags[k][hf] == "o" else 1))
                     nc.tensor.matmul(
-                        zt[:].rearrange("p (t r) -> p t r", t=4), lhsT=ones_b[:],
-                        rhs=ba_rows[:, cols].rearrange("p (r t k) -> p k t r", t=4, k=NBR)[:, k],
+                        zt[:].rearrange("p (t q r) -> p t q r", t=2, r=8), lhsT=ones_b[:],
+                        rhs=ba_rows[:].rearrange("p (q t r k) -> p k t q r", t=4, r=8, k=NBR)[:, k, ts],
                         start=True, stop=False)
                     z[(k, hf)] = zt
                 for k in range(NBR):
                     for kc in range(2):
                         nc.tensor.matmul(
-                            z[(k, hf)][:].rearrange("p (t r) -> p t r", t=4), lhsT=ght[:, kc, :],
-                            rhs=wa[:, kc, cols].rearrange("p (r t k) -> p k t r", t=4, k=NBR)[:, k],
+                            z[(k, hf)][:].rearrange("p (t q r) -> p t q r", t=2, r=8), lhsT=ght[:, kc, :],
+                            rhs=wa[:, kc, :].rearrange("p (q t r k) -> p k t q r", t=4, r=8, k=NBR)[:, k, ts],
                             start=False, stop=(kc == 1))
 
             wo_grp = [head.tile([P, C, 4], BF16, tag="wa", name="wo_grp0", align_bytes=64),

@@ -14,25 +14,29 @@ ACT = mybir.ActivationFunctionType
 P = 128
 B, HW, C, GH, NBR = 128, 25, 1024, 256, 3
 HALF = 512
-XBUFS = 3
-CHUNKS = ((0, 2), (2, 4), (6, 4), (10, 4), (14, 4), (18, 4), (22, 3))
-BLOCKS = ((0, 1), (1, 1)) + tuple((2 + 2 * i, 2) for i in range(11)) + ((24, 1),)
+XBUFS = 5
+CHUNKS = tuple((2 * i, 2) for i in range(12)) + ((24, 1),)
+BLOCKS = ((0, 1), (1, 1)) + tuple((2 + 2 * i, 2) for i in range(10)) + ((22, 1), (23, 1), (24, 1))
 NB = len(BLOCKS)
 
 FLOPS = 2 * B * HW * C * C + 2 * B * GH * NBR * C
 
 
-def by_channel(ap, hf):
-    return ap.rearrange("b n (q t r) -> b t n q r", t=4, r=8)[:, 2 * hf:2 * hf + 2]
+def by_slot(ap):
+    return ap.rearrange("b (t w) -> b t w", t=4)
 
 
-def by_parts(t, hf):
-    return t[:, 2 * hf:2 * hf + 2].rearrange("b t n (q r) -> b t n q r", r=8)
+def by_channel(ap, t0, t1):
+    return ap.rearrange("b n (q t r) -> b t n q r", t=4, r=8)[:, t0:t1]
 
 
-def over_images(ap, n):
-    v = ap.rearrange("b (t q r) -> b t q r", t=2, r=8).unsqueeze(2)
-    return v.to_broadcast([P, 2, n, 32, 8])
+def over_images(ap, t, n):
+    v = ap.rearrange("b (t q r) -> b t q r", t=t, r=8).unsqueeze(2)
+    return v.to_broadcast([P, t, n, 32, 8])
+
+
+PIECES = ((1, 0, 2), (0, 0, 2), (1, 2, 3), (0, 2, 4))
+GPSIMD_PIECES = ((2, 0, 4, 0), (1, 3, 4, 4))
 
 
 def tile_hiremodule_pc_kernel(tc, h_mix, w_mix, c_proj, gate_hid, wa2, ba2, wo, bo, out):
@@ -44,20 +48,22 @@ def tile_hiremodule_pc_kernel(tc, h_mix, w_mix, c_proj, gate_hid, wa2, ba2, wo, 
         ctx.enter_context(tc.manual_schedule())
         consts = ctx.enter_context(tc.tile_pool(name="consts", bufs=1))
         xpool = ctx.enter_context(tc.tile_pool(name="xpool", bufs=XBUFS))
-        ppool = ctx.enter_context(tc.tile_pool(name="ppool", bufs=2))
+        vpool = ctx.enter_context(tc.tile_pool(name="vpool", bufs=2))
+        ppool = ctx.enter_context(tc.tile_pool(name="ppool", bufs=3))
         gpool = ctx.enter_context(tc.tile_pool(name="gpool", bufs=2))
         psum = ctx.enter_context(tc.psum_pool(name="psum", bufs=1))
 
         ident_f = consts.tile([P, P], F32, name="ident_f")
         ident_b = consts.tile([P, P], BF16, name="ident_b")
-        a_sb = consts.tile([P, NBR, C], F32, name="a_sb")
+        a_sb = consts.tile([P, NBR, 4, 2, P], F32, name="a_sb")
         bo_bc = consts.tile([P, C], BF16, name="bo_bc")
         w_codes = consts.tile([P, 2, C], U32, name="w_codes", align_bytes=64)
         w_scales = consts.tile([P, 2, C], U8, name="w_scales", align_bytes=64)
 
         xt = {}
         a_ps = {}
-        prod = {}
+        made_v = {}
+        made_g = {}
         quant = {}
         stage = {}
         pools = {}
@@ -82,40 +88,38 @@ def tile_hiremodule_pc_kernel(tc, h_mix, w_mix, c_proj, gate_hid, wa2, ba2, wo, 
                     return c, ij - i0
             return None
 
-        def new_products(q):
-            n = BLOCKS[q][1]
-            for k in range(NBR):
-                prod[(q, k)] = ppool.tile([P, 4, n, C // 4], F32, tag="p%d" % k, name="p%d_%d" % (k, q))
-
-        def pre_added(q):
-            return BLOCKS[q][1] == 2
-
-        def halves(q):
-            return (1, 0) if pre_added(q) else (0, 1)
-
-        def touch(q):
-            nc.vector.memset(prod[(q, 2)][:, 2 * halves(q)[0], 0, 0:8], 0.0)
+        def vector_slots(q, k, t0, t1):
+            if q not in made_v:
+                made_v[q] = vpool.tile([P, 7, BLOCKS[q][1], C // 4], F32, tag="made_v", name="made_v%d" % q)
+            s0 = t0 + (4 if k == 1 else 0)
+            return made_v[q][:, s0:s0 + t1 - t0].rearrange("b t n (q r) -> b t n q r", r=8)
 
         def gpsimd_share(q):
-            n = BLOCKS[q][1]
             c, j0 = where(BLOCKS[q][0])
-            for hf in halves(q):
+            n = BLOCKS[q][1]
+            made_g[q] = ppool.tile([P, 5, n, C // 4], F32, tag="made_g", name="made_g%d" % q)
+            if q >= 2:
+                nc.vector.memset(made_g[q][:, 0, 0, 0:8], 0.0)
+            for (k, t0, t1, s0) in GPSIMD_PIECES:
                 nc.gpsimd.tensor_tensor(
-                    out=by_parts(prod[(q, 2)], hf), in0=by_channel(xt[(2, c)][:, j0:j0 + n, :], hf),
-                    in1=over_images(a_sb[:, 2, hf * HALF:(hf + 1) * HALF], n), op=ALU.mult)
+                    out=made_g[q][:, s0:s0 + t1 - t0].rearrange("b t n (q r) -> b t n q r", r=8),
+                    in0=by_channel(xt[(k, c)][:, j0:j0 + n, :], t0, t1),
+                    in1=over_images(a_sb[:, k, t0:t1].rearrange("p t g w -> p (t g w)"), t1 - t0, n), op=ALU.mult)
 
-        def gpsimd_add(q):
-            if pre_added(q):
-                nc.gpsimd.tensor_tensor(out=prod[(q, 2)][:, 0:2], in0=prod[(q, 2)][:, 0:2],
-                                        in1=prod[(q, 1)][:, 0:2], op=ALU.add)
-
-        def vector_share(q):
-            n = BLOCKS[q][1]
+        def vector_position(q, jj):
             c, j0 = where(BLOCKS[q][0])
-            for (k, hf) in [(k, hf) for hf in halves(q) for k in (1, 0)]:
+            for (k, t0, t1) in PIECES:
                 nc.vector.tensor_tensor(
-                    out=by_parts(prod[(q, k)], hf), in0=by_channel(xt[(k, c)][:, j0:j0 + n, :], hf),
-                    in1=over_images(a_ps[(k, hf)][:], n), op=ALU.mult)
+                    out=vector_slots(q, k, t0, t1)[:, :, jj:jj + 1],
+                    in0=by_channel(xt[(k, c)][:, j0 + jj:j0 + jj + 1, :], t0, t1),
+                    in1=over_images(a_ps[(k, t0 // 2)][:, 0:(t1 - t0) * 256], t1 - t0, 1), op=ALU.mult)
+
+        def product(q, k, t):
+            if k == 2:
+                return made_g[q][:, t]
+            if (k, t) == (1, 3):
+                return made_g[q][:, 4]
+            return made_v[q][:, t + 4 * k]
 
         def t_run(q, jj, g):
             n = BLOCKS[q][1]
@@ -126,9 +130,9 @@ def tile_hiremodule_pc_kernel(tc, h_mix, w_mix, c_proj, gate_hid, wa2, ba2, wo, 
                     gpool.tile([P, n * 2 * P], U8, tag="scl", name="scl%d" % q, align_bytes=64),
                 )
             acc = psum.tile([P, 4, P], F32, tag="acc", name="acc%d_%d_%d" % (g, q, jj), bufs=2)
-            for t in (2, 3, 0, 1) if pre_added(q) else (0, 1, 2, 3):
-                for k in (2, 0) if (t < 2 and pre_added(q)) else (2, 1, 0):
-                    nc.tensor.matmul(acc[:, t, :], lhsT=prod[(q, k)][:, t, jj, g * P:(g + 1) * P], rhs=ident_f[:],
+            for t in range(4):
+                for k in (2, 1, 0):
+                    nc.tensor.matmul(acc[:, t, :], lhsT=product(q, k, t)[:, jj, g * P:(g + 1) * P], rhs=ident_f[:],
                                      is_transpose=True, start=(k == 2), stop=(k == 0))
             nc.scalar.copy(out=quant[q][0][:, jj, g, :, :], in_=acc[:].rearrange("p t b -> p b t"))
 
@@ -158,27 +162,25 @@ def tile_hiremodule_pc_kernel(tc, h_mix, w_mix, c_proj, gate_hid, wa2, ba2, wo, 
             if (jj, nh) == (n - 1, 1):
                 nc.sync.dma_start(out=outv[:, ij0:ij0 + n, :], in_=stage[q][:])
 
-        z_tags = (("pa", "pb"), ("pc", "pd"), ("o", "o"))
+        a_tags = {(0, 0): "pa", (0, 1): "pb", (1, 0): "pc", (1, 1): "pd"}
 
         with tc.tile_pool(name="head", bufs=1) as head:
             make_identity(nc, ident_b[:])
             make_identity(nc, ident_f[:])
 
-            ba_rows = head.tile([P, NBR * C], BF16, name="ba_rows")
-            nc.vector.memset(ba_rows[:], 0.0)
-            ones_b = head.tile([P, P], BF16, name="ones_b")
-            nc.vector.memset(ones_b[:], 1.0)
-            warm = head.tile([P, 1], F32, name="warm")
-            nc.vector.memset(warm[:], 0.0)
-
             gh = head.tile([P, GH], BF16, name="gh")
             nc.sync.dma_start(out=gh[:], in_=gate_hid)
-            nc.sync.dma_start(out=ba_rows[0:1, :], in_=ba2.rearrange("(o c) -> o c", o=1))
             wa = head.tile([P, 2, NBR * C], BF16, tag="wa", name="wa", align_bytes=64)
             wav = wa2.rearrange("(kc p) c -> p kc c", p=P)
-            for hf in range(2):
-                cols = slice(hf * NBR * HALF, (hf + 1) * NBR * HALF)
-                nc.sync.dma_start(out=wa[:, :, cols], in_=wav[:, :, cols])
+            ba_rows = head.tile([P, NBR * C], BF16, name="ba_rows")
+            ba_row = ba2.rearrange("(o c) -> o c", o=1)
+            for g in range(2):
+                c0 = g * NBR * HALF
+                nc.vector.memset(ba_rows[:, c0:c0 + NBR * HALF].bitcast(U32), 0)
+                nc.sync.dma_start(out=wa[:, :, c0:c0 + NBR * HALF], in_=wav[:, :, c0:c0 + NBR * HALF])
+                for (row, k) in ((0, 1), (32, 0), (64, 2)):
+                    n = NBR * HALF - (k if g == 1 else 0)
+                    nc.sync.dma_start(out=ba_rows[row:row + 1, c0:c0 + n], in_=ba_row[:, c0 + k:c0 + k + n])
             wo_raw = head.tile([P, 2, 4, C], BF16, name="wo_raw")
             wov = wo.rearrange("(g q t r) n -> r g q t n", g=2, t=4, r=8)
             for g in range(2):
@@ -188,31 +190,41 @@ def tile_hiremodule_pc_kernel(tc, h_mix, w_mix, c_proj, gate_hid, wa2, ba2, wo, 
                 load_chunk(c)
             nc.sync.dma_start(out=bo_bc[:], in_=bo.partition_broadcast(P))
 
+            warm = head.tile([P, 1], F32, name="warm")
+            nc.vector.memset(warm[:], 0.0)
             nc.scalar.activation(out=warm[:], in_=warm[:], func=ACT.Exp)
-
-            ght_ps = psum.tile([P, 2, P], BF16, tag="acc", name="ght_ps", bufs=2)
+            sel = head.tile([P, 2, P], BF16, name="sel")
+            nc.vector.memset(sel[:], 0.0)
+            nc.vector.memset(sel[0:1, 0, :], 1.0)
+            nc.vector.memset(sel[32:33, :, :], -1.0)
+            nc.vector.memset(sel[64:65, 1, :], 1.0)
+            ght_ps = psum.tile([P, 2, P], BF16, tag="pa", name="ght_ps")
             for kc in range(2):
                 nc.tensor.transpose(ght_ps[:, kc, :], gh[:, kc * P:(kc + 1) * P], ident_b[:])
             ght = head.tile([P, 2, P], BF16, name="ght")
+            nght = head.tile([P, 2, P], BF16, name="nght")
             nc.vector.tensor_copy(out=ght[:], in_=ght_ps[:])
+            nc.vector.tensor_scalar_mul(out=nght[:], in0=ght_ps[:], scalar1=-1.0)
 
-            z = {}
-            for hf in range(2):
-                ts = slice(2 * hf, 2 * hf + 2)
-                for k in range(NBR):
-                    zt = psum.tile([P, HALF], F32, tag=z_tags[k][hf], name="z%d_%d" % (k, hf),
-                                   bufs=(2 if z_tags[k][hf] == "o" else 1))
-                    nc.tensor.matmul(
-                        zt[:].rearrange("p (t q r) -> p t q r", t=2, r=8), lhsT=ones_b[:],
-                        rhs=ba_rows[:].rearrange("p (q t r k) -> p k t q r", t=4, r=8, k=NBR)[:, k, ts],
-                        start=True, stop=False)
-                    z[(k, hf)] = zt
-                for k in range(NBR):
+            d = {}
+            for g in range(2):
+                cols = slice(g * NBR * HALF, (g + 1) * NBR * HALF)
+
+                def logits(t, k):
+                    return t.rearrange("p (q t r k) -> p k t q r", t=4, r=8, k=NBR)[:, k]
+
+                for k in (1, 2):
+                    dt = psum.tile([P, HALF], F32, tag=("acc", "o")[g], name="d%d_%d" % (k, g), bufs=2)
+                    dv = dt[:].rearrange("p (t q r) -> p t q r", t=4, r=8)
                     for kc in range(2):
-                        nc.tensor.matmul(
-                            z[(k, hf)][:].rearrange("p (t q r) -> p t q r", t=2, r=8), lhsT=ght[:, kc, :],
-                            rhs=wa[:, kc, :].rearrange("p (q t r k) -> p k t q r", t=4, r=8, k=NBR)[:, k, ts],
-                            start=False, stop=(kc == 1))
+                        nc.tensor.matmul(dv, lhsT=ght[:, kc, :], rhs=logits(wa[:, kc, cols], k),
+                                         start=(kc == 0), stop=False)
+                    for kc in range(2):
+                        nc.tensor.matmul(dv, lhsT=nght[:, kc, :], rhs=logits(wa[:, kc, cols], 0),
+                                         start=False, stop=False)
+                    nc.tensor.matmul(dv, lhsT=sel[:, k - 1, :], rhs=logits(ba_rows[:, cols], 0),
+                                     start=False, stop=True)
+                    d[(k, g)] = dt
 
             wo_grp = [head.tile([P, C, 4], BF16, tag="wa", name="wo_grp0", align_bytes=64),
                       head.tile([P, C, 4], BF16, name="wo_grp1", align_bytes=64)]
@@ -222,77 +234,102 @@ def tile_hiremodule_pc_kernel(tc, h_mix, w_mix, c_proj, gate_hid, wa2, ba2, wo, 
                                         in0=wo_raw[:, 1, :, ns].rearrange("p t n -> p n t"),
                                         scalar1=1.0, scalar2=0.0, op0=ALU.mult, op1=ALU.add)
 
+            r1 = {}
+            m = {}
             e = {}
             s = {}
             y = {}
-            mx = {}
-            for hf in range(2):
-                mx[hf] = head.tile([P, HALF], F32, name="m_%d" % hf)
-                nc.scalar.copy(out=mx[hf][:], in_=z[(0, hf)][:])
-            for hf in range(2):
-                m = mx[hf]
-                nc.vector.tensor_tensor(out=m[:], in0=z[(1, hf)][:], in1=m[:], op=ALU.max)
-                nc.vector.tensor_tensor(out=m[:], in0=z[(2, hf)][:], in1=m[:], op=ALU.max)
-                e[hf] = head.tile([P, NBR, HALF], F32, name="e_%d" % hf)
-                for k in range(NBR):
-                    nc.vector.tensor_tensor(out=e[hf][:, k, :], in0=z[(k, hf)][:], in1=m[:], op=ALU.subtract)
-                nc.scalar.activation(out=e[hf][:], in_=e[hf][:], func=ACT.Exp)
-            for hf in range(2):
-                s[hf] = head.tile([P, HALF], F32, name="s_%d" % hf)
-                y[hf] = head.tile([P, HALF], F32, name="y_%d" % hf)
-                nc.vector.tensor_tensor(out=s[hf][:], in0=e[hf][:, 0, :], in1=e[hf][:, 1, :], op=ALU.add)
-                nc.vector.tensor_tensor(out=s[hf][:], in0=s[hf][:], in1=e[hf][:, 2, :], op=ALU.add)
-            for hf in range(2):
-                nc.scalar.activation(out=y[hf][:], in_=s[hf][:], func=ACT.Abs_reciprocal_sqrt)
-                nc.scalar.activation(out=y[hf][:], in_=y[hf][:], func=ACT.Square)
-            nc.vector.quantize_mx(out=w_codes[:, 1, :].bitcast(FP8X4), scales=w_scales[:, 1, :],
-                                  in_=wo_grp[1][:].rearrange("p n t -> p (n t)"))
+            for g in range(2):
+                r1[g] = head.tile([P, HALF], F32, tag="rs%d" % g, name="r1_%d" % g)
+                m[g] = head.tile([P, HALF], F32, name="m_%d" % g)
+                e[g] = head.tile([P, NBR, HALF], F32, name="e_%d" % g)
+            for g in range(2):
+                nc.scalar.activation(out=r1[g][:], in_=d[(1, g)][:], func=ACT.Relu)
+                nc.vector.tensor_tensor(out=m[g][:], in0=d[(2, g)][:], in1=r1[g][:], op=ALU.max)
+                if g == 0:
+                    nc.scalar.activation(out=e[0][:, 0, :], in_=m[0][:], func=ACT.Exp, scale=-1.0)
+                for k in (1, 2):
+                    nc.vector.tensor_tensor(out=e[g][:, k, :], in0=d[(k, g)][:], in1=m[g][:], op=ALU.subtract)
+            nc.scalar.activation(out=e[0][:, 1:3, :], in_=e[0][:, 1:3, :], func=ACT.Exp)
+            nc.scalar.activation(out=e[1][:, 0, :], in_=m[1][:], func=ACT.Exp, scale=-1.0)
+            nc.scalar.activation(out=e[1][:, 1:3, :], in_=e[1][:, 1:3, :], func=ACT.Exp)
+            for g in range(2):
+                s[g] = head.tile([P, HALF], F32, tag="rs%d" % g, name="s_%d" % g)
+                nc.vector.tensor_tensor(out=s[g][:], in0=e[g][:, 1, :], in1=e[g][:, 0, :], op=ALU.add)
+                nc.vector.tensor_tensor(out=s[g][:], in0=s[g][:], in1=e[g][:, 2, :], op=ALU.add)
+            for g in range(2):
+                y[g] = head.tile([P, HALF], F32, name="y_%d" % g)
+                nc.scalar.activation(out=y[g][:], in_=s[g][:], func=ACT.Abs_reciprocal_sqrt)
+                nc.scalar.activation(out=y[g][:], in_=y[g][:], func=ACT.Square)
             for piece in range(4):
                 ns = slice(piece * 256, (piece + 1) * 256)
                 nc.scalar.copy(out=wo_grp[0][:, ns, :], in_=wo_raw[:, 0, :, ns].rearrange("p t n -> p n t"))
 
-            for hf in range(2):
-                hs = slice(hf * HALF, (hf + 1) * HALF)
-                nc.vector.tensor_tensor(out=s[hf][:], in0=s[hf][:], in1=y[hf][:], op=ALU.mult)
-                nc.vector.scalar_tensor_tensor(out=y[hf][:], in0=s[hf][:], scalar=2.0, in1=y[hf][:],
-                                               op0=ALU.subtract, op1=ALU.mult)
-                nc.vector.scalar_tensor_tensor(
-                    out=a_sb[:, :, hs], in0=e[hf][:], scalar=-1.0,
-                    in1=y[hf][:].unsqueeze(1).to_broadcast([P, NBR, HALF]), op0=ALU.mult, op1=ALU.mult)
-                for k in (1, 0):
-                    ap = psum.tile([P, HALF], F32, tag=z_tags[k][hf], name="aps%d_%d" % (k, hf))
-                    nc.tensor.matmul(ap[:], lhsT=ident_f[:], rhs=a_sb[:, k, hs], start=True, stop=True)
-                    a_ps[(k, hf)] = ap
+            for (k, tp) in ((1, 0), (0, 0), (1, 1), (0, 1)):
+                a_ps[(k, tp)] = psum.tile([P, HALF], F32, tag=a_tags[(k, tp)], name="aps%d_%d" % (k, tp))
+            for g in range(2):
+                nc.vector.tensor_tensor(
+                    out=a_sb[:, 1, 0:3, g, :], in0=by_slot(e[g][:, 1, :])[:, 0:3], in1=by_slot(y[g][:])[:, 0:3],
+                    op=ALU.mult)
+                nc.vector.tensor_tensor(
+                    out=a_sb[:, 0, :, g, :], in0=by_slot(e[g][:, 0, :]), in1=by_slot(y[g][:]), op=ALU.mult)
+                nc.gpsimd.tensor_tensor(
+                    out=a_sb[:, 2, :, g, :], in0=by_slot(e[g][:, 2, :]), in1=by_slot(y[g][:]), op=ALU.mult)
+                nc.gpsimd.tensor_tensor(
+                    out=a_sb[:, 1, 3, g, :], in0=e[g][:, 1, 3 * P:], in1=y[g][:, 3 * P:], op=ALU.mult)
+                for (k, tp) in ((1, 0), (0, 0), (1, 1), (0, 1)):
+                    nt = 1 if (k, tp) == (1, 1) else 2
+                    nc.tensor.matmul(a_ps[(k, tp)][:].rearrange("p (t g w) -> p t g w", t=2, g=2)[:, 0:nt, g, :],
+                                     lhsT=ident_f[:], rhs=a_sb[:, k, 2 * tp:2 * tp + nt, g, :],
+                                     start=True, stop=True)
 
             for q in range(2):
-                new_products(q)
                 gpsimd_share(q)
-            for q in range(2):
-                vector_share(q)
-                gpsimd_add(q)
-                load_after(q)
-            nc.vector.quantize_mx(out=w_codes[:, 0, :].bitcast(FP8X4), scales=w_scales[:, 0, :],
-                                  in_=wo_grp[0][:].rearrange("p n t -> p (n t)"))
+            def quantise_wo(g):
+                nc.vector.quantize_mx(out=w_codes[:, g, :].bitcast(FP8X4), scales=w_scales[:, g, :],
+                                      in_=wo_grp[g][:].rearrange("p n t -> p (n t)"))
+
+            for (k, t0, t1) in PIECES:
+                nc.vector.tensor_tensor(
+                    out=vector_slots(0, k, t0, t1)[:, :, 0:1], in0=by_channel(xt[(k, 0)][:, 0:1, :], t0, t1),
+                    in1=over_images(a_sb[:, k, t0:t1].rearrange("p t g w -> p (t g w)"), t1 - t0, 1), op=ALU.mult)
+            for g in (1, 0):
+                nc.vector.quantize_mx(out=w_codes[:, g, :].bitcast(FP8X4), scales=w_scales[:, g, :],
+                                      in_=wo_grp[g][:].rearrange("p n t -> p (n t)"))
 
         pools["o"] = ctx.enter_context(tc.tile_pool(name="opool", bufs=3))
 
-        for q in range(NB + 1):
-            if q < NB:
-                for g in halves(q):
-                    for jj in range(BLOCKS[q][1]):
-                        t_run(q, jj, g)
-            pairs = [(jj, nh) for jj in range(BLOCKS[q - 1][1]) for nh in range(2)] if q >= 1 else []
-            for (jj, nh) in pairs[:2]:
-                add_bias(q - 1, jj, nh, mx_pair(q - 1, jj, nh))
-            if q < NB:
-                quantise(q)
+        sums = {}
+
+        def mx_position(q, jj):
+            for nh in range(2):
+                sums[(q, jj, nh)] = mx_pair(q, jj, nh)
+
+        def bias_position(q, jj):
+            for nh in range(2):
+                add_bias(q, jj, nh, sums[(q, jj, nh)])
+
+        for q in range(NB + 2):
+            if 1 <= q <= NB:
+                quantise(q - 1)
+            if q >= 2:
+                bias_position(q - 2, BLOCKS[q - 2][1] - 1)
             if q + 2 < NB:
-                new_products(q + 2)
-                touch(q + 2)
                 gpsimd_share(q + 2)
-            for (jj, nh) in pairs[2:]:
-                add_bias(q - 1, jj, nh, mx_pair(q - 1, jj, nh))
-            if q + 2 < NB:
-                vector_share(q + 2)
-                gpsimd_add(q + 2)
-                load_after(q + 2)
+            if q < NB:
+                t_run(q, 0, 0)
+                t_run(q, 0, 1)
+            if q + 1 < NB:
+                vector_position(q + 1, 0)
+            if 1 <= q <= NB and BLOCKS[q - 1][1] == 2:
+                mx_position(q - 1, 0)
+                bias_position(q - 1, 0)
+            if q < NB and BLOCKS[q][1] == 2:
+                t_run(q, 1, 0)
+                t_run(q, 1, 1)
+            if q + 1 < NB:
+                if BLOCKS[q + 1][1] == 2:
+                    vector_position(q + 1, 1)
+                load_after(q + 1)
+            if 1 <= q <= NB:
+                mx_position(q - 1, BLOCKS[q - 1][1] - 1)

@@ -301,8 +301,8 @@ def tile_hiremodule_pc_kernel(tc, h_mix, w_mix, c_proj, gate_hid, wa2, ba2, wo, 
 
         sums = {}
 
-        def mx_position(q, jj):
-            for nh in range(2):
+        def mx_half(q, jj, nh):
+            if 0 <= q < NB:
                 sums[(q, jj, nh)] = mx_pair(q, jj, nh)
 
         def bias_position(q, jj):
@@ -316,20 +316,20 @@ def tile_hiremodule_pc_kernel(tc, h_mix, w_mix, c_proj, gate_hid, wa2, ba2, wo, 
                 bias_position(q - 2, BLOCKS[q - 2][1] - 1)
             if q + 2 < NB:
                 gpsimd_share(q + 2)
-            if q < NB:
-                t_run(q, 0, 0)
-                t_run(q, 0, 1)
-            if q + 1 < NB:
-                vector_position(q + 1, 0)
-            if 1 <= q <= NB and BLOCKS[q - 1][1] == 2:
-                mx_position(q - 1, 0)
-                bias_position(q - 1, 0)
-            if q < NB and BLOCKS[q][1] == 2:
-                t_run(q, 1, 0)
-                t_run(q, 1, 1)
-            if q + 1 < NB:
-                if BLOCKS[q + 1][1] == 2:
-                    vector_position(q + 1, 1)
-                load_after(q + 1)
-            if 1 <= q <= NB:
-                mx_position(q - 1, BLOCKS[q - 1][1] - 1)
+            n_t = BLOCKS[q][1] if q < NB else 0
+            n_m = BLOCKS[q - 1][1] if 1 <= q <= NB else 0
+            for jj in range(2):
+                jm = jj - (2 - n_m)
+                for h in range(2):
+                    if jj < n_t:
+                        t_run(q, jj, h)
+                    if jj == 0 and h == 0 and q + 1 < NB:
+                        vector_position(q + 1, 0)
+                    if 0 <= jm < n_m:
+                        mx_half(q - 1, jm, h)
+                if jj == 0 and n_m == 2:
+                    bias_position(q - 1, 0)
+                if jj == 1 and q + 1 < NB:
+                    if BLOCKS[q + 1][1] == 2:
+                        vector_position(q + 1, 1)
+                    load_after(q + 1)

@@ -36,6 +36,8 @@ def over_images(ap, t, n):
 
 
 PIECES = ((1, 0, 2), (0, 0, 2), (1, 2, 3), (0, 2, 4))
+SHARES = {(1, 1): (2, 2), (1, 2): (4, 4), (2, 1): (0, 1, 2, 1), (2, 2): (0, 2, 3, 3)}
+LAG = 5
 GPSIMD_PIECES = ((2, 0, 4, 0), (1, 3, 4, 4))
 
 
@@ -106,13 +108,13 @@ def tile_hiremodule_pc_kernel(tc, h_mix, w_mix, c_proj, gate_hid, wa2, ba2, wo, 
                     in0=by_channel(xt[(k, c)][:, j0:j0 + n, :], t0, t1),
                     in1=over_images(a_sb[:, k, t0:t1].rearrange("p t g w -> p (t g w)"), t1 - t0, n), op=ALU.mult)
 
-        def vector_position(q, jj):
+        def vector_product(q, jj, piece):
+            k, t0, t1 = PIECES[piece]
             c, j0 = where(BLOCKS[q][0])
-            for (k, t0, t1) in PIECES:
-                nc.vector.tensor_tensor(
-                    out=vector_slots(q, k, t0, t1)[:, :, jj:jj + 1],
-                    in0=by_channel(xt[(k, c)][:, j0 + jj:j0 + jj + 1, :], t0, t1),
-                    in1=over_images(a_ps[(k, t0 // 2)][:, 0:(t1 - t0) * 256], t1 - t0, 1), op=ALU.mult)
+            nc.vector.tensor_tensor(
+                out=vector_slots(q, k, t0, t1)[:, :, jj:jj + 1],
+                in0=by_channel(xt[(k, c)][:, j0 + jj:j0 + jj + 1, :], t0, t1),
+                in1=over_images(a_ps[(k, t0 // 2)][:, 0:(t1 - t0) * 256], t1 - t0, 1), op=ALU.mult)
 
         def product(q, k, t):
             if k == 2:
@@ -300,36 +302,41 @@ def tile_hiremodule_pc_kernel(tc, h_mix, w_mix, c_proj, gate_hid, wa2, ba2, wo, 
         pools["o"] = ctx.enter_context(tc.tile_pool(name="opool", bufs=3))
 
         sums = {}
+        block_of = {}
+        for q in range(NB):
+            for jj in range(BLOCKS[q][1]):
+                block_of[BLOCKS[q][0] + jj] = (q, jj)
 
-        def mx_half(q, jj, nh):
-            if 0 <= q < NB:
-                sums[(q, jj, nh)] = mx_pair(q, jj, nh)
+        def vector_work(q, h):
+            if q + 1 >= NB:
+                return
+            n0, n1 = BLOCKS[q][1], BLOCKS[q + 1][1]
+            todo = [(0, 0), (0, 1), (0, 2), (0, 3)] + ([(1, 3), (1, 0), (1, 1), (1, 2)] if n1 == 2 else [])
+            counts = SHARES[(n0, n1)]
+            i0 = sum(counts[0:h])
+            for (jj, piece) in todo[i0:i0 + counts[h]]:
+                vector_product(q + 1, jj, piece)
+            if h == len(counts) - 1:
+                load_after(q + 1)
 
-        def bias_position(q, jj):
-            for nh in range(2):
-                add_bias(q, jj, nh, sums[(q, jj, nh)])
-
-        for q in range(NB + 2):
-            if 1 <= q <= NB:
-                quantise(q - 1)
-            if q >= 2:
-                bias_position(q - 2, BLOCKS[q - 2][1] - 1)
-            if q + 2 < NB:
-                gpsimd_share(q + 2)
-            n_t = BLOCKS[q][1] if q < NB else 0
-            n_m = BLOCKS[q - 1][1] if 1 <= q <= NB else 0
-            for jj in range(2):
-                jm = jj - (2 - n_m)
-                for h in range(2):
-                    if jj < n_t:
-                        t_run(q, jj, h)
-                    if jj == 0 and h == 0 and q + 1 < NB:
-                        vector_position(q + 1, 0)
-                    if 0 <= jm < n_m:
-                        mx_half(q - 1, jm, h)
-                if jj == 0 and n_m == 2:
-                    bias_position(q - 1, 0)
-                if jj == 1 and q + 1 < NB:
-                    if BLOCKS[q + 1][1] == 2:
-                        vector_position(q + 1, 1)
-                    load_after(q + 1)
+        for i in range(2 * HW + LAG + 1):
+            if i < 2 * HW:
+                q, jj = block_of[i // 2]
+                t_run(q, jj, i % 2)
+                if jj == 0 and i % 2 == 0:
+                    if q >= 1:
+                        quantise(q - 1)
+                    if q + 2 < NB:
+                        gpsimd_share(q + 2)
+            elif i == 2 * HW:
+                quantise(NB - 1)
+            done = i - LAG - 1
+            if done >= 0:
+                q_done, jj_done = block_of[done // 2]
+                add_bias(q_done, jj_done, done % 2, sums[done])
+            if i < 2 * HW:
+                vector_work(q, 2 * jj + i % 2)
+            new = i - LAG
+            if 0 <= new < 2 * HW:
+                q_new, jj_new = block_of[new // 2]
+                sums[new] = mx_pair(q_new, jj_new, new % 2)

@@ -160,7 +160,7 @@ def tile_hiremodule_pc_kernel(tc, h_mix, w_mix, c_proj, gate_hid, wa2, ba2, wo, 
             if (jj, nh) == (0, 0):
                 stage[q] = pools["o"].tile([P, n, C], F32, tag="ost", name="ost%d" % q)
             ns = slice(nh * HALF, (nh + 1) * HALF)
-            nc.vector.tensor_tensor(out=stage[q][:, jj, ns], in0=o[:], in1=bo_bc[:, ns], op=ALU.add)
+            nc.vector.tensor_tensor(out=stage[q][:, jj, ns], in0=bo_bc[:, ns], in1=o[:], op=ALU.add)
             if (jj, nh) == (n - 1, 1):
                 nc.sync.dma_start(out=outv[:, ij0:ij0 + n, :], in_=stage[q][:])
 

@@ -35,10 +35,10 @@ def over_images(ap, t, n):
     return v.to_broadcast([P, t, n, 32, 8])
 
 
-PIECES = ((1, 0, 2), (0, 0, 2), (1, 2, 3), (0, 2, 4))
+PIECES = ((1, 0, 2), (0, 0, 2), (1, 2, 4), (0, 2, 4))
 SHARES = {(1, 1): (2, 2), (1, 2): (4, 4), (2, 1): (0, 1, 2, 1), (2, 2): (0, 2, 3, 3)}
 LAG = 5
-GPSIMD_PIECES = ((2, 0, 4, 0), (1, 3, 4, 4))
+GPSIMD_PIECES = ((2, 0, 4, 0),)
 
 
 def tile_hiremodule_pc_kernel(tc, h_mix, w_mix, c_proj, gate_hid, wa2, ba2, wo, bo, out):
@@ -92,14 +92,14 @@ def tile_hiremodule_pc_kernel(tc, h_mix, w_mix, c_proj, gate_hid, wa2, ba2, wo, 
 
         def vector_slots(q, k, t0, t1):
             if q not in made_v:
-                made_v[q] = vpool.tile([P, 7, BLOCKS[q][1], C // 4], F32, tag="made_v", name="made_v%d" % q)
+                made_v[q] = vpool.tile([P, 8, BLOCKS[q][1], C // 4], F32, tag="made_v", name="made_v%d" % q)
             s0 = t0 + (4 if k == 1 else 0)
             return made_v[q][:, s0:s0 + t1 - t0].rearrange("b t n (q r) -> b t n q r", r=8)
 
         def gpsimd_share(q):
             c, j0 = where(BLOCKS[q][0])
             n = BLOCKS[q][1]
-            made_g[q] = ppool.tile([P, 5, n, C // 4], F32, tag="made_g", name="made_g%d" % q)
+            made_g[q] = ppool.tile([P, 4, n, C // 4], F32, tag="made_g", name="made_g%d" % q)
             if q >= 2:
                 nc.vector.memset(made_g[q][:, 0, 0, 0:8], 0.0)
             for (k, t0, t1, s0) in GPSIMD_PIECES:
@@ -119,8 +119,6 @@ def tile_hiremodule_pc_kernel(tc, h_mix, w_mix, c_proj, gate_hid, wa2, ba2, wo, 
         def product(q, k, t):
             if k == 2:
                 return made_g[q][:, t]
-            if (k, t) == (1, 3):
-                return made_g[q][:, 4]
             return made_v[q][:, t + 4 * k]
 
         def t_run(q, jj, g):
@@ -271,18 +269,14 @@ def tile_hiremodule_pc_kernel(tc, h_mix, w_mix, c_proj, gate_hid, wa2, ba2, wo, 
                 a_ps[(k, tp)] = psum.tile([P, HALF], F32, tag=a_tags[(k, tp)], name="aps%d_%d" % (k, tp))
             for g in range(2):
                 nc.vector.tensor_tensor(
-                    out=a_sb[:, 1, 0:3, g, :], in0=by_slot(e[g][:, 1, :])[:, 0:3], in1=by_slot(y[g][:])[:, 0:3],
-                    op=ALU.mult)
+                    out=a_sb[:, 1, :, g, :], in0=by_slot(e[g][:, 1, :]), in1=by_slot(y[g][:]), op=ALU.mult)
                 nc.vector.tensor_tensor(
                     out=a_sb[:, 0, :, g, :], in0=by_slot(e[g][:, 0, :]), in1=by_slot(y[g][:]), op=ALU.mult)
                 nc.gpsimd.tensor_tensor(
                     out=a_sb[:, 2, :, g, :], in0=by_slot(e[g][:, 2, :]), in1=by_slot(y[g][:]), op=ALU.mult)
-                nc.gpsimd.tensor_tensor(
-                    out=a_sb[:, 1, 3, g, :], in0=e[g][:, 1, 3 * P:], in1=y[g][:, 3 * P:], op=ALU.mult)
                 for (k, tp) in ((1, 0), (0, 0), (1, 1), (0, 1)):
-                    nt = 1 if (k, tp) == (1, 1) else 2
-                    nc.tensor.matmul(a_ps[(k, tp)][:].rearrange("p (t g w) -> p t g w", t=2, g=2)[:, 0:nt, g, :],
-                                     lhsT=ident_f[:], rhs=a_sb[:, k, 2 * tp:2 * tp + nt, g, :],
+                    nc.tensor.matmul(a_ps[(k, tp)][:].rearrange("p (t g w) -> p t g w", t=2, g=2)[:, :, g, :],
+                                     lhsT=ident_f[:], rhs=a_sb[:, k, 2 * tp:2 * tp + 2, g, :],
                                      start=True, stop=True)
 
             for q in range(2):

from contextlib import ExitStack

import concourse.mybir as mybir
from concourse.masks import make_identity

F32 = mybir.dt.float32
BF16 = mybir.dt.bfloat16
U32 = mybir.dt.uint32
U8 = mybir.dt.uint8
FP8X4 = mybir.dt.float8_e4m3fn_x4
ALU = mybir.AluOpType
ACT = mybir.ActivationFunctionType

P = 128
B, HW, C, GH, NBR = 128, 25, 1024, 256, 3
HALF = 512
XBUFS = 5
CHUNKS = tuple((2 * i, 2) for i in range(12)) + ((24, 1),)
BLOCKS = ((0, 1), (1, 1)) + tuple((2 + 2 * i, 2) for i in range(10)) + ((22, 1), (23, 1), (24, 1))
NB = len(BLOCKS)

FLOPS = 2 * B * HW * C * C + 2 * B * GH * NBR * C


def by_slot(ap):
    return ap.rearrange("b (t w) -> b t w", t=4)


def by_channel(ap, t0, t1):
    return ap.rearrange("b n (q t r) -> b t n q r", t=4, r=8)[:, t0:t1]


def over_images(ap, t, n):
    v = ap.rearrange("b (t q r) -> b t q r", t=t, r=8).unsqueeze(2)
    return v.to_broadcast([P, t, n, 32, 8])


PIECES = ((1, 0, 2), (0, 0, 2), (1, 2, 4), (0, 2, 4))
SHARES = {(1, 1): (2, 2), (1, 2): (4, 4), (2, 1): (0, 1, 2, 1), (2, 2): (0, 2, 3, 3)}
LAG = 5
GPSIMD_PIECES = ((2, 0, 4, 0),)


def tile_hiremodule_pc_kernel(tc, h_mix, w_mix, c_proj, gate_hid, wa2, ba2, wo, bo, out):
    nc = tc.nc
    xv = [x.rearrange("b i j c -> b (i j) c") for x in (h_mix, w_mix, c_proj)]
    outv = out.rearrange("b i j c -> b (i j) c")

    with ExitStack() as ctx:
        ctx.enter_context(tc.manual_schedule())
        consts = ctx.enter_context(tc.tile_pool(name="consts", bufs=1))
        xpool = ctx.enter_context(tc.tile_pool(name="xpool", bufs=XBUFS))
        vpool = ctx.enter_context(tc.tile_pool(name="vpool", bufs=2))
        ppool = ctx.enter_context(tc.tile_pool(name="ppool", bufs=3))
        gpool = ctx.enter_context(tc.tile_pool(name="gpool", bufs=2))
        psum = ctx.enter_context(tc.psum_pool(name="psum", bufs=1))

        ident_f = consts.tile([P, P], F32, name="ident_f")
        ident_b = consts.tile([P, P], BF16, name="ident_b")
        a_sb = consts.tile([P, NBR, 4, 2, P], F32, name="a_sb")
        bo_bc = consts.tile([P, C], BF16, name="bo_bc")
        w_codes = consts.tile([P, 2, C], U32, name="w_codes", align_bytes=64)
        w_scales = consts.tile([P, 2, C], U8, name="w_scales", align_bytes=64)

        xt = {}
        a_ps = {}
        made_v = {}
        made_g = {}
        quant = {}
        stage = {}
        pools = {}

        def load_chunk(c):
            i0, cn = CHUNKS[c]
            for k in range(NBR):
                t = xpool.tile([P, cn, C], BF16, tag="x%d" % k, name="x%d_%d" % (k, c))
                nc.sync.dma_start(out=t[:], in_=xv[k][:, i0:i0 + cn, :])
                xt[(k, c)] = t

        def load_after(q):
            ij_end = BLOCKS[q][0] + BLOCKS[q][1]
            for c in range(len(CHUNKS) - XBUFS):
                if CHUNKS[c][0] + CHUNKS[c][1] == ij_end:
                    load_chunk(c + XBUFS)

        def where(ij):
            for c in range(len(CHUNKS)):
                i0, cn = CHUNKS[c]
                if i0 <= ij < i0 + cn:
                    return c, ij - i0
            return None

        def vector_slots(q, k, t0, t1):
            if q not in made_v:
                made_v[q] = vpool.tile([P, 8, BLOCKS[q][1], C // 4], F32, tag="made_v", name="made_v%d" % q)
            s0 = t0 + (4 if k == 1 else 0)
            return made_v[q][:, s0:s0 + t1 - t0].rearrange("b t n (q r) -> b t n q r", r=8)

        def gpsimd_share(q):
            c, j0 = where(BLOCKS[q][0])
            n = BLOCKS[q][1]
            made_g[q] = ppool.tile([P, 4, n, C // 4], F32, tag="made_g", name="made_g%d" % q)
            if q >= 2:
                nc.vector.memset(made_g[q][:, 0, 0, 0:8], 0.0)
            for (k, t0, t1, s0) in GPSIMD_PIECES:
                nc.gpsimd.tensor_tensor(
                    out=made_g[q][:, s0:s0 + t1 - t0].rearrange("b t n (q r) -> b t n q r", r=8),
                    in0=by_channel(xt[(k, c)][:, j0:j0 + n, :], t0, t1),
                    in1=over_images(a_sb[:, k, t0:t1].rearrange("p t g w -> p (t g w)"), t1 - t0, n), op=ALU.mult)

        def vector_product(q, jj, piece):
            k, t0, t1 = PIECES[piece]
            c, j0 = where(BLOCKS[q][0])
            nc.vector.tensor_tensor(
                out=vector_slots(q, k, t0, t1)[:, :, jj:jj + 1],
                in0=by_channel(xt[(k, c)][:, j0 + jj:j0 + jj + 1, :], t0, t1),
                in1=over_images(a_ps[(k, t0 // 2)][:, 0:(t1 - t0) * 256], t1 - t0, 1), op=ALU.mult)

        def product(q, k, t):
            if k == 2:
                return made_g[q][:, t]
            return made_v[q][:, t + 4 * k]

        def t_run(q, jj, g):
            n = BLOCKS[q][1]
            if q not in quant:
                quant[q] = (
                    gpool.tile([P, n, 2, P, 4], BF16, tag="grp", name="grp%d" % q, align_bytes=64),
                    gpool.tile([P, n * 2 * P], U32, tag="codes", name="codes%d" % q, align_bytes=64),
                    gpool.tile([P, n * 2 * P], U8, tag="scl", name="scl%d" % q, align_bytes=64),
                )
            acc = psum.tile([P, 4, P], F32, tag="acc", name="acc%d_%d_%d" % (g, q, jj), bufs=2)
            for t in range(4):
                for k in (2, 1, 0):
                    nc.tensor.matmul(acc[:, t, :], lhsT=product(q, k, t)[:, jj, g * P:(g + 1) * P], rhs=ident_f[:],
                                     is_transpose=True, start=(k == 2), stop=(k == 0))
            nc.scalar.copy(out=quant[q][0][:, jj, g, :, :], in_=acc[:].rearrange("p t b -> p b t"))

        def quantise(q):
            grp, codes, scl = quant[q]
            nc.vector.quantize_mx(out=codes[:].bitcast(FP8X4), scales=scl[:],
                                  in_=grp[:].rearrange("p j g b t -> p (j g b t)"))

        def mx_pair(q, jj, nh):
            codes, scl = quant[q][1], quant[q][2]
            ns = slice(nh * HALF, (nh + 1) * HALF)
            o = psum.tile([P, HALF], F32, tag="o", name="o%d_%d_%d" % (nh, q, jj), bufs=2)
            for g in range(2):
                gs = slice((2 * jj + g) * P, (2 * jj + g + 1) * P)
                nc.tensor.matmul_mx(
                    out=o[:], lhsT=codes[:, gs].bitcast(FP8X4), lhsT_scale=scl[:, gs],
                    rhs=w_codes[:, g, ns].bitcast(FP8X4), rhs_scale=w_scales[:, g, ns],
                    start=(g == 0), stop=(g == 1))
            return o

        def add_bias(q, jj, nh, o):
            ij0, n = BLOCKS[q]
            if (jj, nh) == (0, 0):
                stage[q] = pools["o"].tile([P, n, C], F32, tag="ost", name="ost%d" % q)
            ns = slice(nh * HALF, (nh + 1) * HALF)
            nc.vector.tensor_tensor(out=stage[q][:, jj, ns], in0=bo_bc[:, ns], in1=o[:], op=ALU.add)
            if (jj, nh) == (n - 1, 1):
                nc.sync.dma_start(out=outv[:, ij0:ij0 + n, :], in_=stage[q][:])

        a_tags = {(0, 0): "pa", (0, 1): "pb", (1, 0): "pc", (1, 1): "pd"}

        with tc.tile_pool(name="head", bufs=1) as head:
            make_identity(nc, ident_b[:])
            make_identity(nc, ident_f[:])

            gh = head.tile([P, GH], BF16, name="gh")
            nc.sync.dma_start(out=gh[:], in_=gate_hid)
            wa = head.tile([P, 2, NBR * C], BF16, tag="wa", name="wa", align_bytes=64)
            wav = wa2.rearrange("(kc p) c -> p kc c", p=P)
            ba_rows = head.tile([P, NBR * C], BF16, name="ba_rows")
            ba_row = ba2.rearrange("(o c) -> o c", o=1)
            for g in range(2):
                c0 = g * NBR * HALF
                nc.vector.memset(ba_rows[:, c0:c0 + NBR * HALF].bitcast(U32), 0)
                nc.sync.dma_start(out=wa[:, :, c0:c0 + NBR * HALF], in_=wav[:, :, c0:c0 + NBR * HALF])
                for (row, k) in ((0, 1), (32, 0), (64, 2)):
                    n = NBR * HALF - (k if g == 1 else 0)
                    nc.sync.dma_start(out=ba_rows[row:row + 1, c0:c0 + n], in_=ba_row[:, c0 + k:c0 + k + n])
            wo_raw = head.tile([P, 2, 4, C], BF16, name="wo_raw")
            wov = wo.rearrange("(g q t r) n -> r g q t n", g=2, t=4, r=8)
            for g in range(2):
                for r in (0, 4, 1, 5, 2, 6, 3, 7):
                    nc.sync.dma_start(out=wo_raw[r:P:8, g, :, :], in_=wov[r, g])
            for c in range(XBUFS):
                load_chunk(c)
            nc.sync.dma_start(out=bo_bc[:], in_=bo.partition_broadcast(P))

            warm = head.tile([P, 1], F32, name="warm")
            nc.vector.memset(warm[:], 0.0)
            nc.scalar.activation(out=warm[:], in_=warm[:], func=ACT.Exp)
            sel = head.tile([P, 2, P], BF16, name="sel")
            nc.vector.memset(sel[:], 0.0)
            nc.vector.memset(sel[0:1, 0, :], 1.0)
            nc.vector.memset(sel[32:33, :, :], -1.0)
            nc.vector.memset(sel[64:65, 1, :], 1.0)
            ght_ps = psum.tile([P, 2, P], BF16, tag="pa", name="ght_ps")
            for kc in range(2):
                nc.tensor.transpose(ght_ps[:, kc, :], gh[:, kc * P:(kc + 1) * P], ident_b[:])
            ght = head.tile([P, 2, P], BF16, name="ght")
            nght = head.tile([P, 2, P], BF16, name="nght")
            nc.vector.tensor_copy(out=ght[:], in_=ght_ps[:])
            nc.vector.tensor_scalar_mul(out=nght[:], in0=ght_ps[:], scalar1=-1.0)

            d = {}
            for g in range(2):
                cols = slice(g * NBR * HALF, (g + 1) * NBR * HALF)

                def logits(t, k):
                    return t.rearrange("p (q t r k) -> p k t q r", t=4, r=8, k=NBR)[:, k]

                for k in (1, 2):
                    dt = psum.tile([P, HALF], F32, tag=("acc", "o")[g], name="d%d_%d" % (k, g), bufs=2)
                    dv = dt[:].rearrange("p (t q r) -> p t q r", t=4, r=8)
                    for kc in range(2):
                        nc.tensor.matmul(dv, lhsT=ght[:, kc, :], rhs=logits(wa[:, kc, cols], k),
                                         start=(kc == 0), stop=False)
                    for kc in range(2):
                        nc.tensor.matmul(dv, lhsT=nght[:, kc, :], rhs=logits(wa[:, kc, cols], 0),
                                         start=False, stop=False)
                    nc.tensor.matmul(dv, lhsT=sel[:, k - 1, :], rhs=logits(ba_rows[:, cols], 0),
                                     start=False, stop=True)
                    d[(k, g)] = dt

            wo_grp = [head.tile([P, C, 4], BF16, tag="wa", name="wo_grp0", align_bytes=64),
                      head.tile([P, C, 4], BF16, name="wo_grp1", align_bytes=64)]
            for piece in range(4):
                ns = slice(piece * 256, (piece + 1) * 256)
                nc.gpsimd.tensor_scalar(out=wo_grp[1][:, ns, :],
                                        in0=wo_raw[:, 1, :, ns].rearrange("p t n -> p n t"),
                                        scalar1=1.0, scalar2=0.0, op0=ALU.mult, op1=ALU.add)

            r1 = {}
            m = {}
            e = {}
            s = {}
            y = {}
            for g in range(2):
                r1[g] = head.tile([P, HALF], F32, tag="rs%d" % g, name="r1_%d" % g)
                m[g] = head.tile([P, HALF], F32, name="m_%d" % g)
                e[g] = head.tile([P, NBR, HALF], F32, name="e_%d" % g)
            for g in range(2):
                nc.scalar.activation(out=r1[g][:], in_=d[(1, g)][:], func=ACT.Relu)
                nc.vector.tensor_tensor(out=m[g][:], in0=d[(2, g)][:], in1=r1[g][:], op=ALU.max)
                if g == 0:
                    nc.scalar.activation(out=e[0][:, 0, :], in_=m[0][:], func=ACT.Exp, scale=-1.0)
                for k in (1, 2):
                    nc.vector.tensor_tensor(out=e[g][:, k, :], in0=d[(k, g)][:], in1=m[g][:], op=ALU.subtract)
            nc.scalar.activation(out=e[0][:, 1:3, :], in_=e[0][:, 1:3, :], func=ACT.Exp)
            nc.scalar.activation(out=e[1][:, 0, :], in_=m[1][:], func=ACT.Exp, scale=-1.0)
            nc.scalar.activation(out=e[1][:, 1:3, :], in_=e[1][:, 1:3, :], func=ACT.Exp)
            for g in range(2):
                s[g] = head.tile([P, HALF], F32, tag="rs%d" % g, name="s_%d" % g)
                nc.vector.tensor_tensor(out=s[g][:], in0=e[g][:, 1, :], in1=e[g][:, 0, :], op=ALU.add)
                nc.vector.tensor_tensor(out=s[g][:], in0=s[g][:], in1=e[g][:, 2, :], op=ALU.add)
            for g in range(2):
                y[g] = head.tile([P, HALF], F32, name="y_%d" % g)
                nc.scalar.activation(out=y[g][:], in_=s[g][:], func=ACT.Abs_reciprocal_sqrt)
                nc.scalar.activation(out=y[g][:], in_=y[g][:], func=ACT.Square)
            for piece in range(4):
                ns = slice(piece * 256, (piece + 1) * 256)
                nc.scalar.copy(out=wo_grp[0][:, ns, :], in_=wo_raw[:, 0, :, ns].rearrange("p t n -> p n t"))

            for (k, tp) in ((1, 0), (0, 0), (1, 1), (0, 1)):
                a_ps[(k, tp)] = psum.tile([P, HALF], F32, tag=a_tags[(k, tp)], name="aps%d_%d" % (k, tp))
            for g in range(2):
                nc.vector.tensor_tensor(
                    out=a_sb[:, 1, :, g, :], in0=by_slot(e[g][:, 1, :]), in1=by_slot(y[g][:]), op=ALU.mult)
                nc.vector.tensor_tensor(
                    out=a_sb[:, 0, :, g, :], in0=by_slot(e[g][:, 0, :]), in1=by_slot(y[g][:]), op=ALU.mult)
                nc.gpsimd.tensor_tensor(
                    out=a_sb[:, 2, :, g, :], in0=by_slot(e[g][:, 2, :]), in1=by_slot(y[g][:]), op=ALU.mult)
                for (k, tp) in ((1, 0), (0, 0), (1, 1), (0, 1)):
                    nc.tensor.matmul(a_ps[(k, tp)][:].rearrange("p (t g w) -> p t g w", t=2, g=2)[:, :, g, :],
                                     lhsT=ident_f[:], rhs=a_sb[:, k, 2 * tp:2 * tp + 2, g, :],
                                     start=True, stop=True)

            for q in range(2):
                gpsimd_share(q)
            def quantise_wo(g):
                nc.vector.quantize_mx(out=w_codes[:, g, :].bitcast(FP8X4), scales=w_scales[:, g, :],
                                      in_=wo_grp[g][:].rearrange("p n t -> p (n t)"))

            for (k, t0, t1) in PIECES:
                nc.vector.tensor_tensor(
                    out=vector_slots(0, k, t0, t1)[:, :, 0:1], in0=by_channel(xt[(k, 0)][:, 0:1, :], t0, t1),
                    in1=over_images(a_sb[:, k, t0:t1].rearrange("p t g w -> p (t g w)"), t1 - t0, 1), op=ALU.mult)
            for g in (1, 0):
                nc.vector.quantize_mx(out=w_codes[:, g, :].bitcast(FP8X4), scales=w_scales[:, g, :],
                                      in_=wo_grp[g][:].rearrange("p n t -> p (n t)"))

        pools["o"] = ctx.enter_context(tc.tile_pool(name="opool", bufs=3))

        sums = {}
        block_of = {}
        for q in range(NB):
            for jj in range(BLOCKS[q][1]):
                block_of[BLOCKS[q][0] + jj] = (q, jj)

        def vector_work(q, h):
            if q + 1 >= NB:
                return
            n0, n1 = BLOCKS[q][1], BLOCKS[q + 1][1]
            todo = [(0, 0), (0, 1), (0, 2), (0, 3)] + ([(1, 3), (1, 0), (1, 1), (1, 2)] if n1 == 2 else [])
            counts = SHARES[(n0, n1)]
            i0 = sum(counts[0:h])
            for (jj, piece) in todo[i0:i0 + counts[h]]:
                vector_product(q + 1, jj, piece)
            if h == len(counts) - 1:
                load_after(q + 1)

        for i in range(2 * HW + LAG + 1):
            if i < 2 * HW:
                q, jj = block_of[i // 2]
                t_run(q, jj, i % 2)
                if jj == 0 and i % 2 == 0:
                    if q >= 1:
                        quantise(q - 1)
                    if q + 2 < NB:
                        gpsimd_share(q + 2)
            elif i == 2 * HW:
                quantise(NB - 1)
            done = i - LAG - 1
            if done >= 0:
                q_done, jj_done = block_of[done // 2]
                add_bias(q_done, jj_done, done % 2, sums[done])
            if i < 2 * HW:
                vector_work(q, 2 * jj + i % 2)
            new = i - LAG
            if 0 <= new < 2 * HW:
                q_new, jj_new = block_of[new // 2]
                sums[new] = mx_pair(q_new, jj_new, new % 2)
